import numpy as np
import ml_dtypes


def mxq(x, axis, fmt="e4m3"):
    dtype, down = {"e4m3": (ml_dtypes.float8_e4m3fn, 7), "e5m2": (ml_dtypes.float8_e5m2, 14)}[fmt]
    v = np.moveaxis(np.asarray(x, np.float32).astype(ml_dtypes.bfloat16).astype(np.float64), axis, -1)
    blocks = v.reshape(v.shape[:-1] + (-1, 32))
    amax = np.abs(blocks).max(-1, keepdims=True)
    byte = np.maximum(np.where(amax > 0, np.frexp(amax)[1] - 1 + 127, 0) - down, 1)
    scale = np.exp2(byte - 127.0)
    codes = (blocks / scale).astype(np.float32).astype(dtype).astype(np.float64)
    return np.moveaxis((codes * scale).reshape(v.shape), -1, axis)


WIDE = False


def mx_kscale(k):
    if not WIDE:
        return np.ones(k)
    levels = np.array([10, -10, 5, -5, 0])
    if k % 512:
        return np.exp2(np.random.permutation(np.resize(levels, k // 32))).repeat(32)
    a = np.empty((k // 512, 16))
    for p in range(k // 512):
        a[p, :8] = np.random.permutation(np.resize(levels, 8))
        for g in range(8):
            far = levels[np.abs(levels - a[p, g]) >= 10]
            a[p, g + 8] = far[np.random.randint(len(far))]
    return np.exp2(a.ravel()).repeat(32)


BF16 = ml_dtypes.bfloat16


def bf(x):
    return np.asarray(x, np.float32).astype(BF16)


def f64(x):
    return np.asarray(x).astype(np.float64)


B, S, E, H, HKV, D, F, M0, M1 = 2, 4096, 512, 1, 1, 128, 8192, 48, 40
M2 = D - M0 - M1
ROPE_BASE = 1000000.0
EPS = 1e-6


def rms_norm(v, w):
    return w * (v / np.sqrt(np.mean(v * v, axis=-1, keepdims=True) + EPS))


def mrope_cos_sin():
    t = np.arange(S, dtype=np.float64)
    parts = []
    for sd in (M0, M1, M2):
        inv_freq = 1.0 / ROPE_BASE ** (np.arange(0, sd, 2, dtype=np.float64) / sd)
        freqs = t[:, None] * inv_freq[None, :]
        parts.append(np.concatenate([freqs, freqs], -1))
    emb = np.concatenate(parts, -1)
    return np.cos(emb), np.sin(emb)


def rotate_half(v):
    d = D // 2
    return np.concatenate([-v[..., d:], v[..., :d]], -1)


def setup_inputs():
    s = mx_kscale(E)
    row = 0.5 + 1.5 * np.random.random_sample((B, S, 1))
    return {"x": bf(np.random.standard_normal((B, S, E)) * row),
            "ln1_w": bf((1.0 + 0.1 * np.random.standard_normal(E)) * s),
            "wq": bf(np.random.standard_normal((H * D, E)) / np.sqrt(E) / s),
            "wk": bf(np.random.standard_normal((HKV * D, E)) / np.sqrt(E) / s),
            "wv": bf(np.random.standard_normal((HKV * D, E)) / np.sqrt(E) / s),
            "q_norm_w": bf(1.0 + 0.1 * np.random.standard_normal(D)),
            "k_norm_w": bf(1.0 + 0.1 * np.random.standard_normal(D))}


def reference(x, ln1_w, wq, wk, wv, q_norm_w, k_norm_w):
    hq = mxq(rms_norm(f64(x), f64(ln1_w)), 2, "e4m3")
    q = (hq @ mxq(f64(wq), 1, "e4m3").T).reshape(B, S, H, D).transpose(0, 2, 1, 3)
    k = (hq @ mxq(f64(wk), 1, "e4m3").T).reshape(B, S, HKV, D).transpose(0, 2, 1, 3)
    v = (hq @ mxq(f64(wv), 1, "e4m3").T).reshape(B, S, HKV, D).transpose(0, 2, 1, 3)
    q = rms_norm(q, f64(q_norm_w))
    k = rms_norm(k, f64(k_norm_w))
    cos, sin = mrope_cos_sin()
    q = q * cos + rotate_half(q) * sin
    k = k * cos + rotate_half(k) * sin
    return q, k, v

@@ -1,0 +1,429 @@
+import math
+from contextlib import ExitStack
+
+import concourse.mybir as mybir
+from concourse.masks import make_identity
+
+F32 = mybir.dt.float32
+BF16 = mybir.dt.bfloat16
+I32 = mybir.dt.int32
+U32 = mybir.dt.uint32
+U8 = mybir.dt.uint8
+FP8X4 = mybir.dt.float8_e4m3fn_x4
+ACT = mybir.ActivationFunctionType
+ALU = mybir.AluOpType
+
+P = 128
+FLOPS = 2 * 8192 * 512 * 384
+ROPE_BASE = 1000000.0
+EPS = 1e-6
+NCH = 16
+FINE_FROM = 14
+ANGLE_GROUPS = ((0, 8), (8, 24))
+GROUPS = ((0, 4), (4, 4), (8, 8), (16, 8), (24, 8))
+VECTOR_GROUPS = 1
+
+
+def tile_selectivetransformerlayer_pa_t_kernel(
+    tc, x, ln1_w, wq, wk, wv, q_norm_w, k_norm_w, out_0, out_1, out_2
+):
+    nc = tc.nc
+    outs = (out_0, out_1, out_2)
+    with ExitStack() as ctx:
+        const = ctx.enter_context(tc.tile_pool(name="const", bufs=1))
+        xpool = ctx.enter_context(tc.tile_pool(name="xpool", bufs=8))
+        hpool = ctx.enter_context(tc.tile_pool(name="hpool", bufs=3))
+        gpool = ctx.enter_context(tc.tile_pool(name="gpool", bufs=3))
+        ppool = ctx.enter_context(tc.tile_pool(name="ppool", bufs=2))
+        opool = ctx.enter_context(tc.tile_pool(name="opool", bufs=3))
+        small = ctx.enter_context(tc.tile_pool(name="small", bufs=8))
+        junkp = ctx.enter_context(tc.tile_pool(name="junkp", bufs=4))
+        ps_w = ctx.enter_context(tc.psum_pool(name="ps_w", bufs=1))
+        ps_t = ctx.enter_context(tc.psum_pool(name="ps_t", bufs=2))
+        ps_o = ctx.enter_context(tc.psum_pool(name="ps_o", bufs=5))
+        ctx.enter_context(tc.manual_schedule())
+
+        X = {}
+        SS = {}
+        RS = {}
+        H = {}
+        PT = {}
+        GQ = {}
+        CD = {}
+        PO = {}
+        SQ = {}
+        RQ = {}
+        PR = {}
+        OQ = {}
+        OV = {}
+        TAB = {}
+
+        def load(n):
+            ch, b = n // 2, n % 2
+            xt = xpool.tile([P, 4, 512], BF16, name="xt")
+            src = x[b, 512 * ch : 512 * ch + 512, :].rearrange("(p i) c -> p i c", i=4)
+            pieces = 2 if n == 0 else 1
+            w = 4 // pieces
+            for piece in range(pieces):
+                nc.sync.dma_start(
+                    out=xt[:, w * piece : w * piece + w, :],
+                    in_=src[:, w * piece : w * piece + w, :],
+                )
+            X[n] = xt
+
+        ones = const.tile([P, 1], F32, name="ones")
+        nc.vector.memset(ones[:], 1.0)
+        rows = const.tile([P, 768], BF16, name="rows")
+        nc.vector.memset(rows[:], 0.0)
+        sel = const.tile([P, P], BF16, name="sel")
+        nc.vector.memset(sel[:], 0.0)
+        nc.vector.memset(sel[0:1, :], 1.0)
+        pos_i = const.tile([P, 32], I32, name="pos_i")
+        nc.gpsimd.iota(pos_i[:], pattern=[[512, 8], [1, 4]], base=0, channel_multiplier=4)
+        ident = const.tile([P, P], F32, name="ident")
+        make_identity(nc, ident[:])
+
+        load(0)
+        nc.sync.dma_start(out=rows[0:1, 0:512], in_=ln1_w.rearrange("(o n) -> o n", o=1))
+        nc.sync.dma_start(out=rows[0:1, 512:640], in_=q_norm_w.rearrange("(o n) -> o n", o=1))
+        nc.sync.dma_start(out=rows[0:1, 640:768], in_=k_norm_w.rearrange("(o n) -> o n", o=1))
+        w_sb = const.tile([P, 4, 512], BF16, name="w_sb")
+        nc.sync.dma_start(out=w_sb[:, 0, :], in_=wq)
+        nc.sync.dma_start(out=w_sb[0:64, 1, :], in_=wq[0:64, :])
+        nc.sync.dma_start(out=w_sb[64:128, 1, :], in_=wk[0:64, :])
+        nc.sync.dma_start(out=w_sb[0:64, 2, :], in_=wk[64:128, :])
+        nc.sync.dma_start(out=w_sb[64:128, 2, :], in_=wk[0:64, :])
+        nc.sync.dma_start(out=w_sb[:, 3, :], in_=wv)
+        for n in range(1, 4):
+            load(n)
+
+        warm = const.tile([P, 1], F32, name="warm")
+        nc.scalar.activation(out=warm[:], in_=ones[:], func=ACT.Sin)
+
+        rate = const.tile([P, 44], F32, name="rate")
+
+        def times(d0, s0, n, c, src):
+            nc.vector.tensor_scalar(
+                out=rate[:, d0 : d0 + n], in0=src[:, s0 : s0 + n], scalar1=c, scalar2=None, op0=ALU.mult
+            )
+
+        for d0 in (0, 24):
+            times(d0, 0, 1, 1.0 / (2.0 * math.pi), ones)
+        for m in (1, 2, 4, 8, 16):
+            for d0, sd in ((0, 48), (24, 40)):
+                times(d0 + m, d0, min(m, sd // 2 - m), ROPE_BASE ** (-2.0 * m / sd), rate)
+        pos_f = const.tile([P, 32], F32, name="pos_f")
+        nc.vector.tensor_copy(out=pos_f[:], in_=pos_i[:])
+        eps = const.tile([P, 1], F32, name="eps")
+        nc.vector.tensor_scalar(out=eps[:], in0=ones[:], scalar1=EPS, scalar2=None, op0=ALU.mult)
+        half_pi = const.tile([P, 1], F32, name="half_pi")
+        nc.vector.tensor_scalar(
+            out=half_pi[:], in0=ones[:], scalar1=math.pi / 2.0, scalar2=None, op0=ALU.mult
+        )
+
+        frac = const.tile([P, 32, 44], F32, name="frac")
+        trig_s = const.tile([P, 32, 44], F32, name="trig_s")
+        trig_c = const.tile([P, 32, 44], F32, name="trig_c")
+        turns = const.tile([P, 32, 44], F32, name="turns")
+        whole = const.tile([P, 32, 44], I32, name="whole")
+
+        def angles(g):
+            t0, nt = ANGLE_GROUPS[g]
+            t1 = t0 + nt
+            nc.vector.tensor_tensor(
+                out=turns[:, t0:t1, :],
+                in0=pos_f[:, t0:t1].unsqueeze(2).to_broadcast([P, nt, 44]),
+                in1=rate[:].unsqueeze(1).to_broadcast([P, nt, 44]),
+                op=ALU.mult,
+            )
+            nc.vector.tensor_copy(out=whole[:, t0:t1, :], in_=turns[:, t0:t1, :])
+            nc.vector.tensor_tensor(
+                out=frac[:, t0:t1, :],
+                in0=turns[:, t0:t1, :],
+                in1=whole[:, t0:t1, :],
+                op=ALU.subtract,
+            )
+
+        def sines(g):
+            t0, nt = ANGLE_GROUPS[g]
+            t1 = t0 + nt
+            f = frac[:, t0:t1, :]
+            nc.scalar.activation(
+                out=trig_s[:, t0:t1, :], in_=f, func=ACT.Sin, scale=2.0 * math.pi
+            )
+            nc.scalar.activation(out=trig_c[:, t0:t1, :], in_=f, func=ACT.Abs)
+            nc.scalar.activation(
+                out=trig_c[:, t0:t1, :],
+                in_=trig_c[:, t0:t1, :],
+                func=ACT.Sin,
+                scale=-2.0 * math.pi,
+                bias=half_pi[:, 0:1],
+            )
+
+        def squares(n, i):
+            if i == 0:
+                ss = small.tile([P, 4], F32, name="ss")
+                SS[n] = ss
+            junk = junkp.tile([P, 512], BF16, name="junk")
+            nc.scalar.activation(
+                out=junk[:], in_=X[n][:, i, :], func=ACT.Square, accum_out=SS[n][:, i : i + 1]
+            )
+
+        def rstd_root(n):
+            rs = small.tile([P, 4], F32, name="rs")
+            nc.scalar.activation(
+                out=rs[:],
+                in_=SS[n][:],
+                func=ACT.Abs_reciprocal_sqrt,
+                scale=1.0 / 512.0,
+                bias=eps[:, 0:1],
+            )
+            RS[n] = rs
+
+        def normalise(n, i):
+            if i == 0:
+                ht = hpool.tile([P, 4, 512], BF16, name="ht")
+                H[n] = ht
+            nc.vector.scalar_tensor_tensor(
+                out=H[n][:, i, :],
+                in0=X[n][:, i, :],
+                scalar=RS[n][:, i : i + 1],
+                in1=spread[:],
+                op0=ALU.mult,
+                op1=ALU.mult,
+            )
+
+        def transposes(n, hf):
+            pt = ps_t.tile([P, 2, 2, 128], F32, name="pt")
+            PT[(n, hf)] = pt
+            for i2 in range(2):
+                words = H[n][:, 2 * hf + i2, :].bitcast(F32)
+                for u in range(2):
+                    nc.tensor.transpose(
+                        out=pt[:, i2, u, :], in_=words[:, u:256:2], identity=ident[:]
+                    )
+
+        def evacuate(eng_copy, n, hf):
+            if hf == 0:
+                gq = gpool.tile([P, 2048], BF16, name="gq", align_bytes=64)
+                GQ[n] = gq
+            eng_copy(
+                out=GQ[n][:, 1024 * hf : 1024 * hf + 1024]
+                .bitcast(F32)
+                .rearrange("p (i r u) -> p i r u", i=2, u=2),
+                in_=PT[(n, hf)][:].rearrange("p i u r -> p i r u"),
+            )
+
+        def quantise(n):
+            if n == "w":
+                codes = const.tile([P, 512], U32, name="w_codes", align_bytes=64)
+                scl = const.tile([P, 512], U8, name="w_scales", align_bytes=64)
+            else:
+                codes = gpool.tile([P, 512], U32, name="codes", align_bytes=64)
+                scl = gpool.tile([P, 512], U8, name="scl", align_bytes=64)
+            CD[n] = (codes, scl)
+            nc.vector.quantize_mx(out=codes[:].bitcast(FP8X4), scales=scl[:], in_=GQ[n][:])
+
+        def project(n, i):
+            codes, scl = CD[n]
+            w_codes, w_scales = CD["w"]
+            po = ps_o.tile([P, 512], F32, name="po")
+            PO[(n, i)] = po
+            nc.tensor.matmul_mx(
+                out=po[:],
+                lhsT=codes[:, 128 * i : 128 * i + 128].bitcast(FP8X4),
+                lhsT_scale=scl[:, 128 * i : 128 * i + 128],
+                rhs=w_codes[:].bitcast(FP8X4),
+                rhs_scale=w_scales[:],
+                start=True,
+                stop=True,
+            )
+
+        def head_stats(n, i):
+            po = PO[(n, i)]
+            if i == 0:
+                ov = opool.tile([P, 4, 128], F32, name="ov")
+                OV[n] = ov
+                sq = small.tile([P, 4, 2], F32, name="sq")
+                SQ[n] = sq
+            for qk in range(2):
+                junk2 = junkp.tile([P, 128], BF16, name="junk2")
+                nc.scalar.activation(
+                    out=junk2[:],
+                    in_=po[:, 192 * qk : 192 * qk + 128],
+                    func=ACT.Square,
+                    accum_out=SQ[n][:, i, qk : qk + 1],
+                )
+            nc.scalar.copy(out=OV[n][:, i, :], in_=po[:, 384:512])
+
+        def head_root(n, i0, ni):
+            rq = small.tile([P, 4, 2], F32, name="rq")
+            nc.scalar.activation(
+                out=rq[:, i0 : i0 + ni, :],
+                in_=SQ[n][:, i0 : i0 + ni, :],
+                func=ACT.Abs_reciprocal_sqrt,
+                scale=1.0 / 128.0,
+                bias=eps[:, 0:1],
+            )
+            for i in range(i0, i0 + ni):
+                RQ[(n, i)] = rq
+
+        def table_of(tau):
+            for grp, (t0, nt) in enumerate(GROUPS):
+                if t0 <= tau < t0 + nt:
+                    return TAB[grp], tau - t0
+            return None, 0
+
+        def rope_products(n, i):
+            po = PO[(n, i)]
+            rq = RQ[(n, i)]
+            if i == 0:
+                pr = ppool.tile([P, 2, 4, 2, 128], F32, name="pr")
+                PR[n] = pr
+            tab, tl = table_of(4 * (n // 2) + i)
+            for qk in range(2):
+                for ab in range(2):
+                    nc.vector.scalar_tensor_tensor(
+                        out=PR[n][:, qk, i, ab, :],
+                        in0=po[:, 192 * qk + 64 * ab : 192 * qk + 64 * ab + 128],
+                        scalar=rq[:, i, qk : qk + 1],
+                        in1=tab[:, ab, tl, qk, :],
+                        op0=ALU.mult,
+                        op1=ALU.mult,
+                    )
+
+        def rope_add(eng, n, i0, ni):
+            if i0 == 0:
+                oq = opool.tile([P, 2, 4, 128], F32, name="oq")
+                OQ[n] = oq
+            eng.tensor_tensor(
+                out=OQ[n][:, :, i0 : i0 + ni, :],
+                in0=PR[n][:, :, i0 : i0 + ni, 0, :],
+                in1=PR[n][:, :, i0 : i0 + ni, 1, :],
+                op=ALU.add,
+            )
+
+        def store(n, k):
+            ch, b = n // 2, n % 2
+            src_t = OQ[n][:, k, :, :] if k < 2 else OV[n][:]
+            nc.sync.dma_start(
+                out=outs[k][b, 0, 512 * ch : 512 * ch + 512, :].rearrange("(m i) d -> m (i d)", i=4),
+                in_=src_t.rearrange("p i d -> p (i d)"),
+            )
+
+        angles(0)
+        spread = ps_w.tile([P, 512], F32, name="spread")
+        nc.tensor.matmul(out=spread[:], lhsT=sel[:], rhs=rows[:, 0:512], start=True, stop=True)
+        spread_n = ps_o.tile([P, 512], F32, name="po")
+        nc.tensor.matmul(
+            out=spread_n[:, 0:256], lhsT=sel[:], rhs=rows[:, 512:768], start=True, stop=True
+        )
+        sines(0)
+        angles(1)
+        H["w"] = w_sb
+        for hf in range(2):
+            transposes("w", hf)
+        for hf in range(2):
+            evacuate(nc.vector.tensor_copy, "w", hf)
+
+        wn = spread_n[:, 0:256].rearrange("p (q h c) -> p q h c", q=2, h=2)
+        w_cos = const.tile([P, 2, 2, 64], F32, name="w_cos")
+        nc.vector.tensor_copy(out=w_cos[:], in_=wn)
+        w_sin = const.tile([P, 2, 2, 64], F32, name="w_sin")
+        nc.vector.tensor_scalar(
+            out=w_sin[:, :, 0, :], in0=wn[:, :, 1, :], scalar1=-1.0, scalar2=None, op0=ALU.mult
+        )
+        nc.vector.tensor_copy(out=w_sin[:, :, 1, :], in_=wn[:, :, 0, :])
+        quantise("w")
+
+        def fold_ops(grp):
+            t0, nt = GROUPS[grp]
+            tab = const.tile([P, 2, nt, 2, 128], F32, name="tab%d" % grp)
+            TAB[grp] = tab
+            ops = []
+            for ab, (tr, wrow) in enumerate(((trig_c, w_cos), (trig_s, w_sin))):
+                wflat = wrow[:].rearrange("p q h c -> p q (h c)")
+                for qk in range(2):
+                    for c0, reps, d0, nd in ((0, 2, 0, 24), (48, 4, 24, 20)):
+                        ops.append((tab, ab, qk, c0, reps, d0, nd, tr, wflat, t0, nt))
+            return ops
+
+        def fold_one(eng, op):
+            tab, ab, qk, c0, reps, d0, nd, tr, wflat, t0, nt = op
+            eng.tensor_tensor(
+                out=tab[:, ab, :, qk, c0 : c0 + reps * nd].rearrange("p t (r d) -> p t r d", r=reps),
+                in0=tr[:, t0 : t0 + nt, d0 : d0 + nd].unsqueeze(2).to_broadcast([P, nt, reps, nd]),
+                in1=wflat[:, qk, c0 : c0 + reps * nd]
+                .rearrange("p (r d) -> p r d", r=reps)
+                .unsqueeze(1)
+                .to_broadcast([P, nt, reps, nd]),
+                op=ALU.mult,
+            )
+
+        for i in range(4):
+            squares(0, i)
+        sines(1)
+        for grp in range(VECTOR_GROUPS):
+            for op in fold_ops(grp):
+                fold_one(nc.vector, op)
+        pending = []
+        for grp in range(VECTOR_GROUPS, len(GROUPS)):
+            pending.extend(fold_ops(grp))
+        cursor = [0]
+
+        def ok(n):
+            return 0 <= n < NCH
+
+        def folds(count):
+            for rep in range(count):
+                if cursor[0] < len(pending):
+                    fold_one(nc.gpsimd, pending[cursor[0]])
+                    cursor[0] = cursor[0] + 1
+
+        folds(8)
+        rstd_root(0)
+
+        for k in range(-4, NCH):
+            fine = k >= FINE_FROM
+            if k + 7 >= 4 and ok(k + 7):
+                load(k + 7)
+            if ok(k + 1):
+                quantise(k + 1)
+            if ok(k + 4) and k + 4 >= 1:
+                squares(k + 4, 0)
+                squares(k + 4, 1)
+            if ok(k + 2):
+                transposes(k + 2, 0)
+                transposes(k + 2, 1)
+            for i in range(4):
+                if ok(k):
+                    rope_products(k, i)
+                    if k == NCH - 1:
+                        rope_add(nc.vector if i % 2 else nc.gpsimd, k, i, 1)
+                    elif i % 2 == 1:
+                        rope_add(nc.gpsimd, k, i - 1, 2)
+                if ok(k + 1):
+                    project(k + 1, i)
+            if ok(k + 2):
+                evacuate(nc.scalar.copy, k + 2, 0)
+                evacuate(nc.scalar.copy, k + 2, 1)
+            if ok(k + 4) and k + 4 >= 1:
+                squares(k + 4, 2)
+                squares(k + 4, 3)
+                rstd_root(k + 4)
+            if ok(k + 3):
+                for i in range(4):
+                    normalise(k + 3, i)
+            if ok(k + 1):
+                for i in range(4):
+                    head_stats(k + 1, i)
+                    if fine:
+                        head_root(k + 1, i, 1)
+                if not fine:
+                    head_root(k + 1, 0, 4)
+            folds(1 if k < 0 else 2)
+            if ok(k + 1):
+                store(k + 1, 2)
+            if ok(k):
+                store(k, 0)
+                store(k, 1)

@@ -18,10 +18,21 @@ FLOPS = 2 * 8192 * 512 * 384
 ROPE_BASE = 1000000.0
 EPS = 1e-6
 NCH = 16
-FINE_FROM = 14
+NT = 4 * NCH
+FA = 2
+HF = 8
+RSG = 2
+COSG = (0, 0)
+FOLD0 = 1
+EVV = 0
+PRE = 0
+LATE = ()
+EVE = 14
+A1 = 0
+WC = 2
+L_NM = 0
 ANGLE_GROUPS = ((0, 8), (8, 24))
 GROUPS = ((0, 4), (4, 4), (8, 8), (16, 8), (24, 8))
-VECTOR_GROUPS = 1
 
 
 def tile_selectivetransformerlayer_pa_t_kernel(
@@ -34,7 +45,7 @@ def tile_selectivetransformerlayer_pa_t_kernel(
         xpool = ctx.enter_context(tc.tile_pool(name="xpool", bufs=8))
         hpool = ctx.enter_context(tc.tile_pool(name="hpool", bufs=3))
         gpool = ctx.enter_context(tc.tile_pool(name="gpool", bufs=3))
-        ppool = ctx.enter_context(tc.tile_pool(name="ppool", bufs=2))
+        ppool = ctx.enter_context(tc.tile_pool(name="ppool", bufs=4))
         opool = ctx.enter_context(tc.tile_pool(name="opool", bufs=3))
         small = ctx.enter_context(tc.tile_pool(name="small", bufs=8))
         junkp = ctx.enter_context(tc.tile_pool(name="junkp", bufs=4))
@@ -51,6 +62,7 @@ def tile_selectivetransformerlayer_pa_t_kernel(
         GQ = {}
         CD = {}
         PO = {}
+        PV = {}
         SQ = {}
         RQ = {}
         PR = {}
@@ -74,7 +86,7 @@ def tile_selectivetransformerlayer_pa_t_kernel(
         ones = const.tile([P, 1], F32, name="ones")
         nc.vector.memset(ones[:], 1.0)
         rows = const.tile([P, 768], BF16, name="rows")
-        nc.vector.memset(rows[:], 0.0)
+        nc.gpsimd.memset(rows[:], 0.0)
         sel = const.tile([P, P], BF16, name="sel")
         nc.vector.memset(sel[:], 0.0)
         nc.vector.memset(sel[0:1, :], 1.0)
@@ -82,19 +94,18 @@ def tile_selectivetransformerlayer_pa_t_kernel(
         nc.gpsimd.iota(pos_i[:], pattern=[[512, 8], [1, 4]], base=0, channel_multiplier=4)
         ident = const.tile([P, P], F32, name="ident")
         make_identity(nc, ident[:])
+        neg_half = const.tile([P, 4], F32, name="neg_half")
+        nc.gpsimd.memset(neg_half[:], -0.5)
 
         load(0)
+        w_sb = const.tile([P, 3, 512], BF16, name="w_sb")
+        for wi, w in enumerate((wq, wk, wv)):
+            nc.sync.dma_start(out=w_sb[:, wi, :], in_=w)
         nc.sync.dma_start(out=rows[0:1, 0:512], in_=ln1_w.rearrange("(o n) -> o n", o=1))
+        load(1)
         nc.sync.dma_start(out=rows[0:1, 512:640], in_=q_norm_w.rearrange("(o n) -> o n", o=1))
         nc.sync.dma_start(out=rows[0:1, 640:768], in_=k_norm_w.rearrange("(o n) -> o n", o=1))
-        w_sb = const.tile([P, 4, 512], BF16, name="w_sb")
-        nc.sync.dma_start(out=w_sb[:, 0, :], in_=wq)
-        nc.sync.dma_start(out=w_sb[0:64, 1, :], in_=wq[0:64, :])
-        nc.sync.dma_start(out=w_sb[64:128, 1, :], in_=wk[0:64, :])
-        nc.sync.dma_start(out=w_sb[0:64, 2, :], in_=wk[64:128, :])
-        nc.sync.dma_start(out=w_sb[64:128, 2, :], in_=wk[0:64, :])
-        nc.sync.dma_start(out=w_sb[:, 3, :], in_=wv)
-        for n in range(1, 4):
+        for n in range(2, 4):
             load(n)
 
         warm = const.tile([P, 1], F32, name="warm")
@@ -116,6 +127,7 @@ def tile_selectivetransformerlayer_pa_t_kernel(
         nc.vector.tensor_copy(out=pos_f[:], in_=pos_i[:])
         eps = const.tile([P, 1], F32, name="eps")
         nc.vector.tensor_scalar(out=eps[:], in0=ones[:], scalar1=EPS, scalar2=None, op0=ALU.mult)
+
         half_pi = const.tile([P, 1], F32, name="half_pi")
         nc.vector.tensor_scalar(
             out=half_pi[:], in0=ones[:], scalar1=math.pi / 2.0, scalar2=None, op0=ALU.mult
@@ -144,6 +156,13 @@ def tile_selectivetransformerlayer_pa_t_kernel(
                 op=ALU.subtract,
             )
 
+        def cosines(t0, nt):
+            t1 = t0 + nt
+            nc.gpsimd.tensor_tensor(out=trig_c[:, t0:t1, :], in0=half_s[:, t0:t1, :], in1=half_s[:, t0:t1, :], op=ALU.mult)
+            nc.gpsimd.tensor_scalar(out=trig_c[:, t0:t1, :], in0=trig_c[:, t0:t1, :], scalar1=-2.0, scalar2=1.0, op0=ALU.mult, op1=ALU.add)
+
+        half_s = const.tile([P, 32, 44], F32, name="half_s")
+
         def sines(g):
             t0, nt = ANGLE_GROUPS[g]
             t1 = t0 + nt
@@ -151,6 +170,9 @@ def tile_selectivetransformerlayer_pa_t_kernel(
             nc.scalar.activation(
                 out=trig_s[:, t0:t1, :], in_=f, func=ACT.Sin, scale=2.0 * math.pi
             )
+            if COSG[g]:
+                nc.scalar.activation(out=half_s[:, t0:t1, :], in_=f, func=ACT.Sin, scale=math.pi)
+                return
             nc.scalar.activation(out=trig_c[:, t0:t1, :], in_=f, func=ACT.Abs)
             nc.scalar.activation(
                 out=trig_c[:, t0:t1, :],
@@ -180,6 +202,15 @@ def tile_selectivetransformerlayer_pa_t_kernel(
             )
             RS[n] = rs
 
+        def rstd_pow(n):
+            ms = small.tile([P, 4], F32, name="ms")
+            nc.gpsimd.tensor_scalar(
+                out=ms[:], in0=SS[n][:], scalar1=1.0 / 512.0, scalar2=EPS, op0=ALU.mult, op1=ALU.add
+            )
+            rs = small.tile([P, 4], F32, name="rs")
+            nc.gpsimd.tensor_tensor(out=rs[:], in0=ms[:], in1=neg_half[:], op=ALU.pow)
+            RS[n] = rs
+
         def normalise(n, i):
             if i == 0:
                 ht = hpool.tile([P, 4, 512], BF16, name="ht")
@@ -196,7 +227,7 @@ def tile_selectivetransformerlayer_pa_t_kernel(
         def transposes(n, hf):
             pt = ps_t.tile([P, 2, 2, 128], F32, name="pt")
             PT[(n, hf)] = pt
-            for i2 in range(2):
+            for i2 in range(1 if (n, hf) == ("w", 1) else 2):
                 words = H[n][:, 2 * hf + i2, :].bitcast(F32)
                 for u in range(2):
                     nc.tensor.transpose(
@@ -214,13 +245,27 @@ def tile_selectivetransformerlayer_pa_t_kernel(
                 in_=PT[(n, hf)][:].rearrange("p i u r -> p i r u"),
             )
 
+        def copy_weights():
+            gw = const.tile([P, 512, 4], BF16, name="gw", align_bytes=64)
+            GQ["w"] = gw[:].rearrange("p n t -> p (n t)")
+            g = gw[:].rearrange("p n t -> p (n t)").bitcast(F32).rearrange("p (n u) -> p n u", u=2)
+            src = PT[("w", 0)][:].rearrange("p q u r -> p q r u")
+            gqk = g[:, 0:384, :].rearrange("p (q n) u -> p q n u", q=2)
+            nc.vector.tensor_copy(out=gqk[:, :, 0:128, :], in_=src)
+            nc.vector.tensor_copy(out=gqk[:, :, 128:192, :], in_=src[:, :, 0:64, :])
+            nc.vector.tensor_copy(
+                out=g[:, 384:512, :], in_=PT[("w", 1)][:, 0, :, :].rearrange("p u r -> p r u")
+            )
+
+        def quantise_weights():
+            codes = const.tile([P, 512], U32, name="w_codes", align_bytes=64)
+            scl = const.tile([P, 512], U8, name="w_scales", align_bytes=64)
+            CD["w"] = (codes, scl)
+            nc.vector.quantize_mx(out=codes[:].bitcast(FP8X4), scales=scl[:], in_=GQ["w"])
+
         def quantise(n):
-            if n == "w":
-                codes = const.tile([P, 512], U32, name="w_codes", align_bytes=64)
-                scl = const.tile([P, 512], U8, name="w_scales", align_bytes=64)
-            else:
-                codes = gpool.tile([P, 512], U32, name="codes", align_bytes=64)
-                scl = gpool.tile([P, 512], U8, name="scl", align_bytes=64)
+            codes = gpool.tile([P, 512], U32, name="codes", align_bytes=64)
+            scl = gpool.tile([P, 512], U8, name="scl", align_bytes=64)
             CD[n] = (codes, scl)
             nc.vector.quantize_mx(out=codes[:].bitcast(FP8X4), scales=scl[:], in_=GQ[n][:])
 
@@ -277,14 +322,14 @@ def tile_selectivetransformerlayer_pa_t_kernel(
         def rope_products(n, i):
             po = PO[(n, i)]
             rq = RQ[(n, i)]
-            if i == 0:
-                pr = ppool.tile([P, 2, 4, 2, 128], F32, name="pr")
-                PR[n] = pr
+            if i % 2 == 0:
+                pr = ppool.tile([P, 2, 2, 2, 128], F32, name="pr")
+                PR[(n, i // 2)] = pr
             tab, tl = table_of(4 * (n // 2) + i)
             for qk in range(2):
                 for ab in range(2):
                     nc.vector.scalar_tensor_tensor(
-                        out=PR[n][:, qk, i, ab, :],
+                        out=PR[(n, i // 2)][:, qk, i % 2, ab, :],
                         in0=po[:, 192 * qk + 64 * ab : 192 * qk + 64 * ab + 128],
                         scalar=rq[:, i, qk : qk + 1],
                         in1=tab[:, ab, tl, qk, :],
@@ -298,43 +343,44 @@ def tile_selectivetransformerlayer_pa_t_kernel(
                 OQ[n] = oq
             eng.tensor_tensor(
                 out=OQ[n][:, :, i0 : i0 + ni, :],
-                in0=PR[n][:, :, i0 : i0 + ni, 0, :],
-                in1=PR[n][:, :, i0 : i0 + ni, 1, :],
+                in0=PR[(n, i0 // 2)][:, :, i0 % 2 : i0 % 2 + ni, 0, :],
+                in1=PR[(n, i0 // 2)][:, :, i0 % 2 : i0 % 2 + ni, 1, :],
                 op=ALU.add,
             )
 
-        def store(n, k):
+        def store(n, k, i0=0, ni=4):
             ch, b = n // 2, n % 2
             src_t = OQ[n][:, k, :, :] if k < 2 else OV[n][:]
             nc.sync.dma_start(
-                out=outs[k][b, 0, 512 * ch : 512 * ch + 512, :].rearrange("(m i) d -> m (i d)", i=4),
-                in_=src_t.rearrange("p i d -> p (i d)"),
+                out=outs[k][b, 0, 512 * ch : 512 * ch + 512, :].rearrange("(m i) d -> m i d", i=4)[
+                    :, i0 : i0 + ni, :
+                ],
+                in_=src_t[:, i0 : i0 + ni, :],
             )
 
         angles(0)
+        sines(0)
+        if A1 == 0:
+            angles(1)
         spread = ps_w.tile([P, 512], F32, name="spread")
         nc.tensor.matmul(out=spread[:], lhsT=sel[:], rhs=rows[:, 0:512], start=True, stop=True)
         spread_n = ps_o.tile([P, 512], F32, name="po")
         nc.tensor.matmul(
             out=spread_n[:, 0:256], lhsT=sel[:], rhs=rows[:, 512:768], start=True, stop=True
         )
-        sines(0)
-        angles(1)
-        H["w"] = w_sb
-        for hf in range(2):
-            transposes("w", hf)
-        for hf in range(2):
-            evacuate(nc.vector.tensor_copy, "w", hf)
-
         wn = spread_n[:, 0:256].rearrange("p (q h c) -> p q h c", q=2, h=2)
         w_cos = const.tile([P, 2, 2, 64], F32, name="w_cos")
-        nc.vector.tensor_copy(out=w_cos[:], in_=wn)
         w_sin = const.tile([P, 2, 2, 64], F32, name="w_sin")
-        nc.vector.tensor_scalar(
-            out=w_sin[:, :, 0, :], in0=wn[:, :, 1, :], scalar1=-1.0, scalar2=None, op0=ALU.mult
-        )
-        nc.vector.tensor_copy(out=w_sin[:, :, 1, :], in_=wn[:, :, 0, :])
-        quantise("w")
+
+        def norm_weights():
+            nc.vector.tensor_copy(out=w_cos[:], in_=wn)
+            nc.vector.tensor_scalar(
+                out=w_sin[:, :, 0, :], in0=wn[:, :, 1, :], scalar1=-1.0, scalar2=None, op0=ALU.mult
+            )
+            nc.vector.tensor_copy(out=w_sin[:, :, 1, :], in_=wn[:, :, 0, :])
+
+        if WC < 0:
+            norm_weights()
 
         def fold_ops(grp):
             t0, nt = GROUPS[grp]
@@ -360,39 +406,75 @@ def tile_selectivetransformerlayer_pa_t_kernel(
                 op=ALU.mult,
             )
 
-        for i in range(4):
-            squares(0, i)
-        sines(1)
-        for grp in range(VECTOR_GROUPS):
-            for op in fold_ops(grp):
-                fold_one(nc.vector, op)
         pending = []
-        for grp in range(VECTOR_GROUPS, len(GROUPS)):
-            pending.extend(fold_ops(grp))
+        for grp, (t0, nt) in enumerate(GROUPS):
+            if grp >= 2 and COSG[1]:
+                pending.append((t0, nt))
+            if grp >= 1 or FOLD0 is None:
+                pending.extend(fold_ops(grp))
         cursor = [0]
-
-        def ok(n):
-            return 0 <= n < NCH
 
         def folds(count):
             for rep in range(count):
                 if cursor[0] < len(pending):
-                    fold_one(nc.gpsimd, pending[cursor[0]])
+                    op = pending[cursor[0]]
+                    if len(op) == 2:
+                        cosines(op[0], op[1])
+                    else:
+                        fold_one(nc.gpsimd, op)
                     cursor[0] = cursor[0] + 1
 
-        folds(8)
-        rstd_root(0)
+        H["w"] = w_sb
+        for hf in range(2):
+            transposes("w", hf)
+        if A1 == 1:
+            angles(1)
 
-        for k in range(-4, NCH):
-            fine = k >= FINE_FROM
-            if k + 7 >= 4 and ok(k + 7):
-                load(k + 7)
+        def ok(n):
+            return 0 <= n < NCH
+
+        def sq(n, half):
+            for i in (2 * half, 2 * half + 1):
+                squares(n, i)
+            if half:
+                if n < RSG:
+                    rstd_pow(n)
+                else:
+                    rstd_root(n)
+
+        load(4)
+        load(5)
+        for half in range(2):
+            sq(0, half)
+        if COSG[0]:
+            cosines(0, 8)
+        for half in range(2):
+            sq(1, half)
+        sines(1)
+        for i in range(4):
+            normalise(0, i)
+        copy_weights()
+        norm_weights()
+        quantise_weights()
+        if FOLD0 is not None:
+            for op in fold_ops(0):
+                fold_one(nc.vector, op)
+        folds(HF)
+        if PRE:
+            transposes(0, 0)
+            transposes(0, 1)
+            evacuate(nc.scalar.copy, 0, 0)
+            evacuate(nc.scalar.copy, 0, 1)
+        for k in range(-2, NCH):
+            fine = k >= NCH - 2
+            if k + 8 >= 6 and ok(k + 8):
+                load(k + 8)
             if ok(k + 1):
                 quantise(k + 1)
-            if ok(k + 4) and k + 4 >= 1:
-                squares(k + 4, 0)
-                squares(k + 4, 1)
-            if ok(k + 2):
+            late = k in LATE
+            if ok(k + 4) and not late:
+                sq(k + 4, 0)
+            if ok(k + 2) and not (PRE and k == -2):
                 transposes(k + 2, 0)
                 transposes(k + 2, 1)
             for i in range(4):
@@ -404,13 +486,11 @@ def tile_selectivetransformerlayer_pa_t_kernel(
                         rope_add(nc.gpsimd, k, i - 1, 2)
                 if ok(k + 1):
                     project(k + 1, i)
-            if ok(k + 2):
+            if ok(k + 2) and not (PRE and k == -2):
                 evacuate(nc.scalar.copy, k + 2, 0)
-                evacuate(nc.scalar.copy, k + 2, 1)
-            if ok(k + 4) and k + 4 >= 1:
-                squares(k + 4, 2)
-                squares(k + 4, 3)
-                rstd_root(k + 4)
+                evacuate(nc.vector.tensor_copy if (EVV and 2 <= k + 2 < EVE and (k + 2) % EVV == 0) else nc.scalar.copy, k + 2, 1)
+            if ok(k + 4) and not late:
+                sq(k + 4, 1)
             if ok(k + 3):
                 for i in range(4):
                     normalise(k + 3, i)
@@ -421,9 +501,17 @@ def tile_selectivetransformerlayer_pa_t_kernel(
                         head_root(k + 1, i, 1)
                 if not fine:
                     head_root(k + 1, 0, 4)
-            folds(1 if k < 0 else 2)
+            if ok(k + 4) and late:
+                sq(k + 4, 0)
+                sq(k + 4, 1)
+            folds(FA)
             if ok(k + 1):
                 store(k + 1, 2)
             if ok(k):
-                store(k, 0)
-                store(k, 1)
+                if k == NCH - 1:
+                    for i0 in (0, 2):
+                        for kk in (0, 1):
+                            store(k, kk, i0, 2)
+                else:
+                    store(k, 0)
+                    store(k, 1)

@@ -22,15 +22,22 @@ NT = 4 * NCH
 FA = 2
 HF = 8
 RSG = 2
-COSG = (0, 0)
+COSG = (1, 0)
 FOLD0 = 1
-EVV = 0
+EVV = 4
 PRE = 0
 LATE = ()
 EVE = 14
 A1 = 0
 WC = 2
 L_NM = 0
+HR1 = 0
+HR2 = 1
+QP = 0
+SORD = 0
+GP = 0
+VORD = 0
+V_COPIES = ()
 ANGLE_GROUPS = ((0, 8), (8, 24))
 GROUPS = ((0, 4), (4, 4), (8, 8), (16, 8), (24, 8))
 
@@ -299,7 +306,8 @@ def tile_selectivetransformerlayer_pa_t_kernel(
                     func=ACT.Square,
                     accum_out=SQ[n][:, i, qk : qk + 1],
                 )
-            nc.scalar.copy(out=OV[n][:, i, :], in_=po[:, 384:512])
+            if i not in V_COPIES:
+                nc.scalar.copy(out=OV[n][:, i, :], in_=po[:, 384:512])
 
         def head_root(n, i0, ni):
             rq = small.tile([P, 4, 2], F32, name="rq")
@@ -359,7 +367,6 @@ def tile_selectivetransformerlayer_pa_t_kernel(
             )
 
         angles(0)
-        sines(0)
         if A1 == 0:
             angles(1)
         spread = ps_w.tile([P, 512], F32, name="spread")
@@ -446,6 +453,7 @@ def tile_selectivetransformerlayer_pa_t_kernel(
         load(5)
         for half in range(2):
             sq(0, half)
+        sines(0)
         if COSG[0]:
             cosines(0, 8)
         for half in range(2):
@@ -469,45 +477,81 @@ def tile_selectivetransformerlayer_pa_t_kernel(
             fine = k >= NCH - 2
             if k + 8 >= 6 and ok(k + 8):
                 load(k + 8)
-            if ok(k + 1):
-                quantise(k + 1)
             late = k in LATE
-            if ok(k + 4) and not late:
-                sq(k + 4, 0)
+
+            def s_sq(half):
+                if ok(k + 4) and not late:
+                    sq(k + 4, half)
+
+            def s_ev(hf):
+                if ok(k + 2) and not (PRE and k == -2):
+                    ve = hf == 1 and EVV and 2 <= k + 2 < EVE and (k + 2) % EVV == 0
+                    evacuate(nc.vector.tensor_copy if ve else nc.scalar.copy, k + 2, hf)
+
+            def s_hs():
+                if ok(k + 1):
+                    for i in range(4):
+                        head_stats(k + 1, i)
+                        if fine or HR1:
+                            head_root(k + 1, i, 1)
+                        elif HR2 and i % 2:
+                            head_root(k + 1, i - 1, 2)
+                    if not fine and not HR1 and not HR2:
+                        head_root(k + 1, 0, 4)
+
+            def v_nm(i):
+                if ok(k + 3):
+                    normalise(k + 3, i)
+
+            if QP == 0 and ok(k + 1):
+                quantise(k + 1)
+            if SORD == 0:
+                s_sq(0)
             if ok(k + 2) and not (PRE and k == -2):
                 transposes(k + 2, 0)
                 transposes(k + 2, 1)
             for i in range(4):
                 if ok(k):
                     rope_products(k, i)
+                    if i in V_COPIES:
+                        nc.vector.tensor_copy(out=OV[k][:, i, :], in_=PO[(k, i)][:, 384:512])
                     if k == NCH - 1:
                         rope_add(nc.vector if i % 2 else nc.gpsimd, k, i, 1)
+                    elif GP == 1:
+                        rope_add(nc.gpsimd, k, i, 1)
                     elif i % 2 == 1:
                         rope_add(nc.gpsimd, k, i - 1, 2)
                 if ok(k + 1):
                     project(k + 1, i)
-            if ok(k + 2) and not (PRE and k == -2):
-                evacuate(nc.scalar.copy, k + 2, 0)
-                evacuate(nc.vector.tensor_copy if (EVV and 2 <= k + 2 < EVE and (k + 2) % EVV == 0) else nc.scalar.copy, k + 2, 1)
-            if ok(k + 4) and not late:
-                sq(k + 4, 1)
-            if ok(k + 3):
+                if VORD == 1 and i == 1:
+                    v_nm(0)
+                    v_nm(1)
+                if VORD == 2:
+                    v_nm(i)
+            if SORD == 2:
+                s_sq(0)
+            s_ev(0)
+            s_ev(1)
+            if SORD == 1:
+                s_sq(0)
+            if SORD != 3:
+                s_sq(1)
+            if VORD == 0:
                 for i in range(4):
-                    normalise(k + 3, i)
-            if ok(k + 1):
-                for i in range(4):
-                    head_stats(k + 1, i)
-                    if fine:
-                        head_root(k + 1, i, 1)
-                if not fine:
-                    head_root(k + 1, 0, 4)
+                    v_nm(i)
+            elif VORD == 1:
+                v_nm(2)
+                v_nm(3)
+            s_hs()
+            if SORD == 3:
+                s_sq(0)
+                s_sq(1)
             if ok(k + 4) and late:
                 sq(k + 4, 0)
                 sq(k + 4, 1)
             folds(FA)
-            if ok(k + 1):
-                store(k + 1, 2)
             if ok(k):
+                store(k, 2)
                 if k == NCH - 1:
                     for i0 in (0, 2):
                         for kk in (0, 1):

import math
from contextlib import ExitStack

import concourse.mybir as mybir
from concourse.masks import make_identity

F32 = mybir.dt.float32
BF16 = mybir.dt.bfloat16
I32 = mybir.dt.int32
U32 = mybir.dt.uint32
U8 = mybir.dt.uint8
FP8X4 = mybir.dt.float8_e4m3fn_x4
ACT = mybir.ActivationFunctionType
ALU = mybir.AluOpType

P = 128
FLOPS = 2 * 8192 * 512 * 384
ROPE_BASE = 1000000.0
EPS = 1e-6
NCH = 16
NT = 4 * NCH
FA = 2
HF = 8
RSG = 2
COSG = (1, 0)
FOLD0 = 1
EVV = 4
PRE = 0
LATE = ()
EVE = 14
A1 = 0
WC = 2
L_NM = 0
HR1 = 0
HR2 = 1
QP = 0
SORD = 0
GP = 0
VORD = 0
V_COPIES = ()
ANGLE_GROUPS = ((0, 8), (8, 24))
GROUPS = ((0, 4), (4, 4), (8, 8), (16, 8), (24, 8))


def tile_selectivetransformerlayer_pa_t_kernel(
    tc, x, ln1_w, wq, wk, wv, q_norm_w, k_norm_w, out_0, out_1, out_2
):
    nc = tc.nc
    outs = (out_0, out_1, out_2)
    with ExitStack() as ctx:
        const = ctx.enter_context(tc.tile_pool(name="const", bufs=1))
        xpool = ctx.enter_context(tc.tile_pool(name="xpool", bufs=8))
        hpool = ctx.enter_context(tc.tile_pool(name="hpool", bufs=3))
        gpool = ctx.enter_context(tc.tile_pool(name="gpool", bufs=3))
        ppool = ctx.enter_context(tc.tile_pool(name="ppool", bufs=4))
        opool = ctx.enter_context(tc.tile_pool(name="opool", bufs=3))
        small = ctx.enter_context(tc.tile_pool(name="small", bufs=8))
        junkp = ctx.enter_context(tc.tile_pool(name="junkp", bufs=4))
        ps_w = ctx.enter_context(tc.psum_pool(name="ps_w", bufs=1))
        ps_t = ctx.enter_context(tc.psum_pool(name="ps_t", bufs=2))
        ps_o = ctx.enter_context(tc.psum_pool(name="ps_o", bufs=5))
        ctx.enter_context(tc.manual_schedule())

        X = {}
        SS = {}
        RS = {}
        H = {}
        PT = {}
        GQ = {}
        CD = {}
        PO = {}
        PV = {}
        SQ = {}
        RQ = {}
        PR = {}
        OQ = {}
        OV = {}
        TAB = {}

        def load(n):
            ch, b = n // 2, n % 2
            xt = xpool.tile([P, 4, 512], BF16, name="xt")
            src = x[b, 512 * ch : 512 * ch + 512, :].rearrange("(p i) c -> p i c", i=4)
            pieces = 2 if n == 0 else 1
            w = 4 // pieces
            for piece in range(pieces):
                nc.sync.dma_start(
                    out=xt[:, w * piece : w * piece + w, :],
                    in_=src[:, w * piece : w * piece + w, :],
                )
            X[n] = xt

        ones = const.tile([P, 1], F32, name="ones")
        nc.vector.memset(ones[:], 1.0)
        rows = const.tile([P, 768], BF16, name="rows")
        nc.gpsimd.memset(rows[:], 0.0)
        sel = const.tile([P, P], BF16, name="sel")
        nc.vector.memset(sel[:], 0.0)
        nc.vector.memset(sel[0:1, :], 1.0)
        pos_i = const.tile([P, 32], I32, name="pos_i")
        nc.gpsimd.iota(pos_i[:], pattern=[[512, 8], [1, 4]], base=0, channel_multiplier=4)
        ident = const.tile([P, P], F32, name="ident")
        make_identity(nc, ident[:])
        neg_half = const.tile([P, 4], F32, name="neg_half")
        nc.gpsimd.memset(neg_half[:], -0.5)

        load(0)
        w_sb = const.tile([P, 3, 512], BF16, name="w_sb")
        for wi, w in enumerate((wq, wk, wv)):
            nc.sync.dma_start(out=w_sb[:, wi, :], in_=w)
        nc.sync.dma_start(out=rows[0:1, 0:512], in_=ln1_w.rearrange("(o n) -> o n", o=1))
        load(1)
        nc.sync.dma_start(out=rows[0:1, 512:640], in_=q_norm_w.rearrange("(o n) -> o n", o=1))
        nc.sync.dma_start(out=rows[0:1, 640:768], in_=k_norm_w.rearrange("(o n) -> o n", o=1))
        for n in range(2, 4):
            load(n)

        warm = const.tile([P, 1], F32, name="warm")
        nc.scalar.activation(out=warm[:], in_=ones[:], func=ACT.Sin)

        rate = const.tile([P, 44], F32, name="rate")

        def times(d0, s0, n, c, src):
            nc.vector.tensor_scalar(
                out=rate[:, d0 : d0 + n], in0=src[:, s0 : s0 + n], scalar1=c, scalar2=None, op0=ALU.mult
            )

        for d0 in (0, 24):
            times(d0, 0, 1, 1.0 / (2.0 * math.pi), ones)
        for m in (1, 2, 4, 8, 16):
            for d0, sd in ((0, 48), (24, 40)):
                times(d0 + m, d0, min(m, sd // 2 - m), ROPE_BASE ** (-2.0 * m / sd), rate)
        pos_f = const.tile([P, 32], F32, name="pos_f")
        nc.vector.tensor_copy(out=pos_f[:], in_=pos_i[:])
        eps = const.tile([P, 1], F32, name="eps")
        nc.vector.tensor_scalar(out=eps[:], in0=ones[:], scalar1=EPS, scalar2=None, op0=ALU.mult)

        half_pi = const.tile([P, 1], F32, name="half_pi")
        nc.vector.tensor_scalar(
            out=half_pi[:], in0=ones[:], scalar1=math.pi / 2.0, scalar2=None, op0=ALU.mult
        )

        frac = const.tile([P, 32, 44], F32, name="frac")
        trig_s = const.tile([P, 32, 44], F32, name="trig_s")
        trig_c = const.tile([P, 32, 44], F32, name="trig_c")
        turns = const.tile([P, 32, 44], F32, name="turns")
        whole = const.tile([P, 32, 44], I32, name="whole")

        def angles(g):
            t0, nt = ANGLE_GROUPS[g]
            t1 = t0 + nt
            nc.vector.tensor_tensor(
                out=turns[:, t0:t1, :],
                in0=pos_f[:, t0:t1].unsqueeze(2).to_broadcast([P, nt, 44]),
                in1=rate[:].unsqueeze(1).to_broadcast([P, nt, 44]),
                op=ALU.mult,
            )
            nc.vector.tensor_copy(out=whole[:, t0:t1, :], in_=turns[:, t0:t1, :])
            nc.vector.tensor_tensor(
                out=frac[:, t0:t1, :],
                in0=turns[:, t0:t1, :],
                in1=whole[:, t0:t1, :],
                op=ALU.subtract,
            )

        def cosines(t0, nt):
            t1 = t0 + nt
            nc.gpsimd.tensor_tensor(out=trig_c[:, t0:t1, :], in0=half_s[:, t0:t1, :], in1=half_s[:, t0:t1, :], op=ALU.mult)
            nc.gpsimd.tensor_scalar(out=trig_c[:, t0:t1, :], in0=trig_c[:, t0:t1, :], scalar1=-2.0, scalar2=1.0, op0=ALU.mult, op1=ALU.add)

        half_s = const.tile([P, 32, 44], F32, name="half_s")

        def sines(g):
            t0, nt = ANGLE_GROUPS[g]
            t1 = t0 + nt
            f = frac[:, t0:t1, :]
            nc.scalar.activation(
                out=trig_s[:, t0:t1, :], in_=f, func=ACT.Sin, scale=2.0 * math.pi
            )
            if COSG[g]:
                nc.scalar.activation(out=half_s[:, t0:t1, :], in_=f, func=ACT.Sin, scale=math.pi)
                return
            nc.scalar.activation(out=trig_c[:, t0:t1, :], in_=f, func=ACT.Abs)
            nc.scalar.activation(
                out=trig_c[:, t0:t1, :],
                in_=trig_c[:, t0:t1, :],
                func=ACT.Sin,
                scale=-2.0 * math.pi,
                bias=half_pi[:, 0:1],
            )

        def squares(n, i):
            if i == 0:
                ss = small.tile([P, 4], F32, name="ss")
                SS[n] = ss
            junk = junkp.tile([P, 512], BF16, name="junk")
            nc.scalar.activation(
                out=junk[:], in_=X[n][:, i, :], func=ACT.Square, accum_out=SS[n][:, i : i + 1]
            )

        def rstd_root(n):
            rs = small.tile([P, 4], F32, name="rs")
            nc.scalar.activation(
                out=rs[:],
                in_=SS[n][:],
                func=ACT.Abs_reciprocal_sqrt,
                scale=1.0 / 512.0,
                bias=eps[:, 0:1],
            )
            RS[n] = rs

        def rstd_pow(n):
            ms = small.tile([P, 4], F32, name="ms")
            nc.gpsimd.tensor_scalar(
                out=ms[:], in0=SS[n][:], scalar1=1.0 / 512.0, scalar2=EPS, op0=ALU.mult, op1=ALU.add
            )
            rs = small.tile([P, 4], F32, name="rs")
            nc.gpsimd.tensor_tensor(out=rs[:], in0=ms[:], in1=neg_half[:], op=ALU.pow)
            RS[n] = rs

        def normalise(n, i):
            if i == 0:
                ht = hpool.tile([P, 4, 512], BF16, name="ht")
                H[n] = ht
            nc.vector.scalar_tensor_tensor(
                out=H[n][:, i, :],
                in0=X[n][:, i, :],
                scalar=RS[n][:, i : i + 1],
                in1=spread[:],
                op0=ALU.mult,
                op1=ALU.mult,
            )

        def transposes(n, hf):
            pt = ps_t.tile([P, 2, 2, 128], F32, name="pt")
            PT[(n, hf)] = pt
            for i2 in range(1 if (n, hf) == ("w", 1) else 2):
                words = H[n][:, 2 * hf + i2, :].bitcast(F32)
                for u in range(2):
                    nc.tensor.transpose(
                        out=pt[:, i2, u, :], in_=words[:, u:256:2], identity=ident[:]
                    )

        def evacuate(eng_copy, n, hf):
            if hf == 0:
                gq = gpool.tile([P, 2048], BF16, name="gq", align_bytes=64)
                GQ[n] = gq
            eng_copy(
                out=GQ[n][:, 1024 * hf : 1024 * hf + 1024]
                .bitcast(F32)
                .rearrange("p (i r u) -> p i r u", i=2, u=2),
                in_=PT[(n, hf)][:].rearrange("p i u r -> p i r u"),
            )

        def copy_weights():
            gw = const.tile([P, 512, 4], BF16, name="gw", align_bytes=64)
            GQ["w"] = gw[:].rearrange("p n t -> p (n t)")
            g = gw[:].rearrange("p n t -> p (n t)").bitcast(F32).rearrange("p (n u) -> p n u", u=2)
            src = PT[("w", 0)][:].rearrange("p q u r -> p q r u")
            gqk = g[:, 0:384, :].rearrange("p (q n) u -> p q n u", q=2)
            nc.vector.tensor_copy(out=gqk[:, :, 0:128, :], in_=src)
            nc.vector.tensor_copy(out=gqk[:, :, 128:192, :], in_=src[:, :, 0:64, :])
            nc.vector.tensor_copy(
                out=g[:, 384:512, :], in_=PT[("w", 1)][:, 0, :, :].rearrange("p u r -> p r u")
            )

        def quantise_weights():
            codes = const.tile([P, 512], U32, name="w_codes", align_bytes=64)
            scl = const.tile([P, 512], U8, name="w_scales", align_bytes=64)
            CD["w"] = (codes, scl)
            nc.vector.quantize_mx(out=codes[:].bitcast(FP8X4), scales=scl[:], in_=GQ["w"])

        def quantise(n):
            codes = gpool.tile([P, 512], U32, name="codes", align_bytes=64)
            scl = gpool.tile([P, 512], U8, name="scl", align_bytes=64)
            CD[n] = (codes, scl)
            nc.vector.quantize_mx(out=codes[:].bitcast(FP8X4), scales=scl[:], in_=GQ[n][:])

        def project(n, i):
            codes, scl = CD[n]
            w_codes, w_scales = CD["w"]
            po = ps_o.tile([P, 512], F32, name="po")
            PO[(n, i)] = po
            nc.tensor.matmul_mx(
                out=po[:],
                lhsT=codes[:, 128 * i : 128 * i + 128].bitcast(FP8X4),
                lhsT_scale=scl[:, 128 * i : 128 * i + 128],
                rhs=w_codes[:].bitcast(FP8X4),
                rhs_scale=w_scales[:],
                start=True,
                stop=True,
            )

        def head_stats(n, i):
            po = PO[(n, i)]
            if i == 0:
                ov = opool.tile([P, 4, 128], F32, name="ov")
                OV[n] = ov
                sq = small.tile([P, 4, 2], F32, name="sq")
                SQ[n] = sq
            for qk in range(2):
                junk2 = junkp.tile([P, 128], BF16, name="junk2")
                nc.scalar.activation(
                    out=junk2[:],
                    in_=po[:, 192 * qk : 192 * qk + 128],
                    func=ACT.Square,
                    accum_out=SQ[n][:, i, qk : qk + 1],
                )
            if i not in V_COPIES:
                nc.scalar.copy(out=OV[n][:, i, :], in_=po[:, 384:512])

        def head_root(n, i0, ni):
            rq = small.tile([P, 4, 2], F32, name="rq")
            nc.scalar.activation(
                out=rq[:, i0 : i0 + ni, :],
                in_=SQ[n][:, i0 : i0 + ni, :],
                func=ACT.Abs_reciprocal_sqrt,
                scale=1.0 / 128.0,
                bias=eps[:, 0:1],
            )
            for i in range(i0, i0 + ni):
                RQ[(n, i)] = rq

        def table_of(tau):
            for grp, (t0, nt) in enumerate(GROUPS):
                if t0 <= tau < t0 + nt:
                    return TAB[grp], tau - t0
            return None, 0

        def rope_products(n, i):
            po = PO[(n, i)]
            rq = RQ[(n, i)]
            if i % 2 == 0:
                pr = ppool.tile([P, 2, 2, 2, 128], F32, name="pr")
                PR[(n, i // 2)] = pr
            tab, tl = table_of(4 * (n // 2) + i)
            for qk in range(2):
                for ab in range(2):
                    nc.vector.scalar_tensor_tensor(
                        out=PR[(n, i // 2)][:, qk, i % 2, ab, :],
                        in0=po[:, 192 * qk + 64 * ab : 192 * qk + 64 * ab + 128],
                        scalar=rq[:, i, qk : qk + 1],
                        in1=tab[:, ab, tl, qk, :],
                        op0=ALU.mult,
                        op1=ALU.mult,
                    )

        def rope_add(eng, n, i0, ni):
            if i0 == 0:
                oq = opool.tile([P, 2, 4, 128], F32, name="oq")
                OQ[n] = oq
            eng.tensor_tensor(
                out=OQ[n][:, :, i0 : i0 + ni, :],
                in0=PR[(n, i0 // 2)][:, :, i0 % 2 : i0 % 2 + ni, 0, :],
                in1=PR[(n, i0 // 2)][:, :, i0 % 2 : i0 % 2 + ni, 1, :],
                op=ALU.add,
            )

        def store(n, k, i0=0, ni=4):
            ch, b = n // 2, n % 2
            src_t = OQ[n][:, k, :, :] if k < 2 else OV[n][:]
            nc.sync.dma_start(
                out=outs[k][b, 0, 512 * ch : 512 * ch + 512, :].rearrange("(m i) d -> m i d", i=4)[
                    :, i0 : i0 + ni, :
                ],
                in_=src_t[:, i0 : i0 + ni, :],
            )

        angles(0)
        if A1 == 0:
            angles(1)
        spread = ps_w.tile([P, 512], F32, name="spread")
        nc.tensor.matmul(out=spread[:], lhsT=sel[:], rhs=rows[:, 0:512], start=True, stop=True)
        spread_n = ps_o.tile([P, 512], F32, name="po")
        nc.tensor.matmul(
            out=spread_n[:, 0:256], lhsT=sel[:], rhs=rows[:, 512:768], start=True, stop=True
        )
        wn = spread_n[:, 0:256].rearrange("p (q h c) -> p q h c", q=2, h=2)
        w_cos = const.tile([P, 2, 2, 64], F32, name="w_cos")
        w_sin = const.tile([P, 2, 2, 64], F32, name="w_sin")

        def norm_weights():
            nc.vector.tensor_copy(out=w_cos[:], in_=wn)
            nc.vector.tensor_scalar(
                out=w_sin[:, :, 0, :], in0=wn[:, :, 1, :], scalar1=-1.0, scalar2=None, op0=ALU.mult
            )
            nc.vector.tensor_copy(out=w_sin[:, :, 1, :], in_=wn[:, :, 0, :])

        if WC < 0:
            norm_weights()

        def fold_ops(grp):
            t0, nt = GROUPS[grp]
            tab = const.tile([P, 2, nt, 2, 128], F32, name="tab%d" % grp)
            TAB[grp] = tab
            ops = []
            for ab, (tr, wrow) in enumerate(((trig_c, w_cos), (trig_s, w_sin))):
                wflat = wrow[:].rearrange("p q h c -> p q (h c)")
                for qk in range(2):
                    for c0, reps, d0, nd in ((0, 2, 0, 24), (48, 4, 24, 20)):
                        ops.append((tab, ab, qk, c0, reps, d0, nd, tr, wflat, t0, nt))
            return ops

        def fold_one(eng, op):
            tab, ab, qk, c0, reps, d0, nd, tr, wflat, t0, nt = op
            eng.tensor_tensor(
                out=tab[:, ab, :, qk, c0 : c0 + reps * nd].rearrange("p t (r d) -> p t r d", r=reps),
                in0=tr[:, t0 : t0 + nt, d0 : d0 + nd].unsqueeze(2).to_broadcast([P, nt, reps, nd]),
                in1=wflat[:, qk, c0 : c0 + reps * nd]
                .rearrange("p (r d) -> p r d", r=reps)
                .unsqueeze(1)
                .to_broadcast([P, nt, reps, nd]),
                op=ALU.mult,
            )

        pending = []
        for grp, (t0, nt) in enumerate(GROUPS):
            if grp >= 2 and COSG[1]:
                pending.append((t0, nt))
            if grp >= 1 or FOLD0 is None:
                pending.extend(fold_ops(grp))
        cursor = [0]

        def folds(count):
            for rep in range(count):
                if cursor[0] < len(pending):
                    op = pending[cursor[0]]
                    if len(op) == 2:
                        cosines(op[0], op[1])
                    else:
                        fold_one(nc.gpsimd, op)
                    cursor[0] = cursor[0] + 1

        H["w"] = w_sb
        for hf in range(2):
            transposes("w", hf)
        if A1 == 1:
            angles(1)

        def ok(n):
            return 0 <= n < NCH

        def sq(n, half):
            for i in (2 * half, 2 * half + 1):
                squares(n, i)
            if half:
                if n < RSG:
                    rstd_pow(n)
                else:
                    rstd_root(n)

        load(4)
        load(5)
        for half in range(2):
            sq(0, half)
        sines(0)
        if COSG[0]:
            cosines(0, 8)
        for half in range(2):
            sq(1, half)
        sines(1)
        for i in range(4):
            normalise(0, i)
        copy_weights()
        norm_weights()
        quantise_weights()
        if FOLD0 is not None:
            for op in fold_ops(0):
                fold_one(nc.vector, op)
        folds(HF)
        if PRE:
            transposes(0, 0)
            transposes(0, 1)
            evacuate(nc.scalar.copy, 0, 0)
            evacuate(nc.scalar.copy, 0, 1)
        for k in range(-2, NCH):
            fine = k >= NCH - 2
            if k + 8 >= 6 and ok(k + 8):
                load(k + 8)
            late = k in LATE

            def s_sq(half):
                if ok(k + 4) and not late:
                    sq(k + 4, half)

            def s_ev(hf):
                if ok(k + 2) and not (PRE and k == -2):
                    ve = hf == 1 and EVV and 2 <= k + 2 < EVE and (k + 2) % EVV == 0
                    evacuate(nc.vector.tensor_copy if ve else nc.scalar.copy, k + 2, hf)

            def s_hs():
                if ok(k + 1):
                    for i in range(4):
                        head_stats(k + 1, i)
                        if fine or HR1:
                            head_root(k + 1, i, 1)
                        elif HR2 and i % 2:
                            head_root(k + 1, i - 1, 2)
                    if not fine and not HR1 and not HR2:
                        head_root(k + 1, 0, 4)

            def v_nm(i):
                if ok(k + 3):
                    normalise(k + 3, i)

            if QP == 0 and ok(k + 1):
                quantise(k + 1)
            if SORD == 0:
                s_sq(0)
            if ok(k + 2) and not (PRE and k == -2):
                transposes(k + 2, 0)
                transposes(k + 2, 1)
            for i in range(4):
                if ok(k):
                    rope_products(k, i)
                    if i in V_COPIES:
                        nc.vector.tensor_copy(out=OV[k][:, i, :], in_=PO[(k, i)][:, 384:512])
                    if k == NCH - 1:
                        rope_add(nc.vector if i % 2 else nc.gpsimd, k, i, 1)
                    elif GP == 1:
                        rope_add(nc.gpsimd, k, i, 1)
                    elif i % 2 == 1:
                        rope_add(nc.gpsimd, k, i - 1, 2)
                if ok(k + 1):
                    project(k + 1, i)
                if VORD == 1 and i == 1:
                    v_nm(0)
                    v_nm(1)
                if VORD == 2:
                    v_nm(i)
            if SORD == 2:
                s_sq(0)
            s_ev(0)
            s_ev(1)
            if SORD == 1:
                s_sq(0)
            if SORD != 3:
                s_sq(1)
            if VORD == 0:
                for i in range(4):
                    v_nm(i)
            elif VORD == 1:
                v_nm(2)
                v_nm(3)
            s_hs()
            if SORD == 3:
                s_sq(0)
                s_sq(1)
            if ok(k + 4) and late:
                sq(k + 4, 0)
                sq(k + 4, 1)
            folds(FA)
            if ok(k):
                store(k, 2)
                if k == NCH - 1:
                    for i0 in (0, 2):
                        for kk in (0, 1):
                            store(k, kk, i0, 2)
                else:
                    store(k, 0)
                    store(k, 1)
